import numpy as np
import ml_dtypes


def mxq(x, axis, fmt="e4m3"):
    dtype, down = {"e4m3": (ml_dtypes.float8_e4m3fn, 7), "e5m2": (ml_dtypes.float8_e5m2, 14)}[fmt]
    v = np.moveaxis(np.asarray(x, np.float32).astype(ml_dtypes.bfloat16).astype(np.float64), axis, -1)
    blocks = v.reshape(v.shape[:-1] + (-1, 32))
    amax = np.abs(blocks).max(-1, keepdims=True)
    byte = np.maximum(np.where(amax > 0, np.frexp(amax)[1] - 1 + 127, 0) - down, 1)
    scale = np.exp2(byte - 127.0)
    codes = (blocks / scale).astype(np.float32).astype(dtype).astype(np.float64)
    return np.moveaxis((codes * scale).reshape(v.shape), -1, axis)


WIDE = False


def mx_kscale(k):
    if not WIDE:
        return np.ones(k)
    levels = np.array([10, -10, 5, -5, 0])
    if k % 512:
        return np.exp2(np.random.permutation(np.resize(levels, k // 32))).repeat(32)
    a = np.empty((k // 512, 16))
    for p in range(k // 512):
        a[p, :8] = np.random.permutation(np.resize(levels, 8))
        for g in range(8):
            far = levels[np.abs(levels - a[p, g]) >= 10]
            a[p, g + 8] = far[np.random.randint(len(far))]
    return np.exp2(a.ravel()).repeat(32)


BF16 = ml_dtypes.bfloat16


def bf(x):
    return np.asarray(x, np.float32).astype(BF16)


def f64(x):
    return np.asarray(x).astype(np.float64)


B, S, D, H, KV, HD, QB = 8, 1024, 512, 2, 2, 64, 512
HALF = HD // 2
THETA = 10000.0


def rope_tables():
    inv_freq = 1.0 / THETA ** (np.arange(HALF) / HALF)
    ang = np.outer(np.random.randint(0, S) + np.arange(S), inv_freq)
    return np.cos(ang)[None, :, None, :], np.sin(ang)[None, :, None, :]


def apply_rope(x, cos, sin):
    xr = x[..., ::2]
    xi = x[..., 1::2]
    rr = xr * cos - xi * sin
    ri = xr * sin + xi * cos
    return np.stack([rr, ri], axis=-1).reshape(x.shape)


def draw0():
    s = mx_kscale(D)
    cos, sin = rope_tables()
    return {"hidden_state": bf(np.random.standard_normal((B, S, D)) * s),
            "freq_cos": bf(cos),
            "freq_sin": bf(sin),
            "wq": bf(np.random.standard_normal((D, H * HD)) * 1.5 / np.sqrt(D) / s[:, None]),
            "wk": bf(np.random.standard_normal((D, KV * HD)) * 1.5 / np.sqrt(D) / s[:, None]),
            "wv": bf(np.random.standard_normal((D, KV * HD)) / np.sqrt(D) / s[:, None])}


def core(hidden_state, freq_cos, freq_sin, wq, wk, wv):
    xq = mxq(f64(hidden_state), 2, "e4m3")
    cos, sin = f64(freq_cos), f64(freq_sin)
    q = (xq @ mxq(f64(wq), 0, "e4m3")).reshape(B, S, H, HD)
    k = (xq @ mxq(f64(wk), 0, "e4m3")).reshape(B, S, KV, HD)
    v = (xq @ mxq(f64(wv), 0, "e4m3")).reshape(B, S, KV, HD)
    return apply_rope(q, cos, sin), apply_rope(k, cos, sin), v


def e4m3fn_bytes(y):
    return np.clip(np.asarray(y, np.float64), -448.0, 448.0).astype(np.float32).astype(ml_dtypes.float8_e4m3fn).view(np.uint8)


def e4m3fn_values(b):
    return np.asarray(b, np.uint8).view(ml_dtypes.float8_e4m3fn).astype(np.float64)


def setup_inputs():
    d = draw0()
    x0 = np.asarray(d['hidden_state']).astype(np.float64)
    s = (np.max(np.abs(x0), axis=(0, 1), keepdims=True) / 448.0).astype(np.float32)
    out = {}
    for k, v in d.items():
        if k == 'hidden_state':
            out['hidden_state_bytes'] = e4m3fn_bytes(x0 / s.astype(np.float64))
            out['hidden_state_scale'] = s
        else:
            out[k] = v
    return out


def reference(hidden_state_bytes, hidden_state_scale, freq_cos, freq_sin, wq, wk, wv):
    return core(e4m3fn_values(hidden_state_bytes) * hidden_state_scale.astype(np.float64), freq_cos, freq_sin, wq, wk, wv)

@@ -1,0 +1,251 @@
+from contextlib import ExitStack
+
+import concourse.mybir as mybir
+from concourse.masks import make_identity
+
+F32 = mybir.dt.float32
+BF16 = mybir.dt.bfloat16
+U32 = mybir.dt.uint32
+U8 = mybir.dt.uint8
+FP8 = mybir.dt.float8_e4m3fn
+FP8X4 = mybir.dt.float8_e4m3fn_x4
+MULT = mybir.AluOpType.mult
+ADD = mybir.AluOpType.add
+COPY = mybir.ActivationFunctionType.Copy
+
+B, S, D = 8, 1024, 512
+HEADS, HD = 2, 64
+HALF = HD // 2
+P = 128
+NG = S // P
+NQK = 256
+NV = 128
+GG = 4
+NBANK = B // 2
+NSTEP = NG * NBANK
+COS_ENGINE = ("gpsimd", "vector", "scalar", "vector")
+TAIL = NSTEP - 6
+
+FLOPS = 2 * B * S * D * (NQK + NV)
+
+
+def tile_attention_pa_t_kernel(
+    tc, hidden_state_bytes, hidden_state_scale, freq_cos, freq_sin, wq, wk, wv, out_0, out_1, out_2
+):
+    nc = tc.nc
+    with ExitStack() as ctx:
+        const = ctx.enter_context(tc.tile_pool(name="const", bufs=1))
+        work = ctx.enter_context(tc.tile_pool(name="work", bufs=2))
+        psum = ctx.enter_context(tc.psum_pool(name="psum", bufs=2))
+
+        warm = const.tile([P, 2], F32, name="warm")
+        nc.vector.memset(warm[:, 0:1], 0.0)
+        nc.scalar.copy(out=warm[:, 1:2], in_=warm[:, 0:1])
+
+        x_view = hidden_state_bytes.rearrange("b (g p) k -> g p b k", p=P)
+        xbytes = []
+        for g in range(NG):
+            xb = const.tile([P, B, D], U8, name="xbytes%d" % g)
+            xbytes.append(xb)
+        sck = const.tile([P, 4], F32, name="sck")
+        w_raw = const.tile([P, 3, 4, 128], BF16, name="w_raw")
+        cos_raw = const.tile([P, NG, HALF], BF16, name="cos_raw")
+        sin_raw = const.tile([P, NG, HALF], BF16, name="sin_raw")
+        nc.sync.dma_start(out=xbytes[0][:, 0:2, :], in_=x_view[0][:, 0:2, :])
+        nc.sync.dma_start(out=sck[:], in_=hidden_state_scale.rearrange("a b (p t) -> (a b p) t", t=4))
+        nc.sync.dma_start(out=xbytes[0][:, 2:4, :], in_=x_view[0][:, 2:4, :])
+        for m, w in enumerate((wq, wk, wv)):
+            nc.sync.dma_start(out=w_raw[:, m], in_=w.rearrange("(p t) n -> p t n", t=4))
+        nc.sync.dma_start(out=xbytes[0][:, 4:8, :], in_=x_view[0][:, 4:8, :])
+        nc.sync.dma_start(
+            out=cos_raw[:], in_=freq_cos.rearrange("a s c j -> (a s) (c j)").rearrange("(g p) j -> p g j", p=P)
+        )
+        nc.sync.dma_start(
+            out=sin_raw[:], in_=freq_sin.rearrange("a s c j -> (a s) (c j)").rearrange("(g p) j -> p g j", p=P)
+        )
+        for g in range(1, NG):
+            nc.sync.dma_start(out=xbytes[g][:], in_=x_view[g])
+
+        ident = const.tile([P, P], F32, name="ident")
+        make_identity(nc, ident[:])
+
+        w_grouped = const.tile([P, 3, 128, 4], BF16, name="w_grouped", align_bytes=64)
+        nc.vector.tensor_copy(out=w_grouped[:], in_=w_raw[:].rearrange("p m t n -> p m n t"))
+        w_flat = w_grouped[:].rearrange("p m n t -> p (m n t)")
+        wcodes = const.tile([P, NQK + NV], U32, name="wcodes", align_bytes=64)
+        wscale = const.tile([P, NQK + NV], U8, name="wscale", align_bytes=64)
+
+        cos2 = const.tile([P, NG * HALF, 2], F32, name="cos2")
+        rot = const.tile([P, NG * HALF, 2], F32, name="rot")
+        cos_flat = cos_raw[:].rearrange("p g j -> p (g j)")
+        sin_flat = sin_raw[:].rearrange("p g j -> p (g j)")
+        nc.gpsimd.tensor_copy(out=cos2[:], in_=cos_flat.unsqueeze(2).to_broadcast([P, NG * HALF, 2]))
+        nc.gpsimd.tensor_scalar(out=rot[:, :, 0], in0=sin_flat, scalar1=-1.0, scalar2=0.0, op0=MULT, op1=ADD)
+        nc.gpsimd.tensor_copy(out=rot[:, :, 1], in_=sin_flat)
+
+        outs_view = []
+        for o in (out_0, out_1, out_2):
+            outs_view.append(o.rearrange("b (g p) h d -> g p b (h d)", p=P))
+        sck_b = sck[:].rearrange("p (u e) -> p u e", u=2).unsqueeze(1).to_broadcast([P, 2 * P, 2, 2])
+
+        xs, xt, grouped, codes, xscale, acc, vacc, t1, t2, y, vsb = {}, {}, {}, {}, {}, {}, {}, {}, {}, {}, {}
+
+        def cast(s):
+            g, q = divmod(s, NBANK)
+            xs[s] = work.tile([P, 2 * D], BF16, name="xs", tag="xs", bufs=4)
+            xb_flat = xbytes[g][:].rearrange("p b k -> p (b k)")
+            nc.scalar.copy(out=xs[s][:], in_=xb_flat[:, q * 2 * D : (q + 1) * 2 * D].bitcast(FP8))
+
+        def transposes(s):
+            xt[s] = psum.tile([P, 2, 2, P], F32, name="xt", tag="xt", bufs=4)
+            words = xs[s][:].bitcast(F32)
+            for tt in range(2):
+                for u in range(2):
+                    nc.tensor.transpose(xt[s][:, u, tt, :], words[:, tt * 256 + u : (tt + 1) * 256 : 2], ident[:])
+
+        def exit_scale(s):
+            g, q = divmod(s, NBANK)
+            if q == 0:
+                grouped[g] = work.tile([P, B * P * 4], BF16, name="grouped", tag="grouped", bufs=3, align_bytes=64)
+            nc.vector.tensor_tensor(
+                out=grouped[g][:, q * 8 * P : (q + 1) * 8 * P].rearrange("p (r u e) -> p r u e", u=2, e=2),
+                in0=xt[s][:].bitcast(BF16).rearrange("p u t (r e) -> p (t r) u e", e=2),
+                in1=sck_b,
+                op=MULT,
+            )
+
+        def quantize(g):
+            codes[g] = work.tile([P, B * P], U32, name="codes", tag="codes", bufs=3, align_bytes=64)
+            xscale[g] = work.tile([P, B * P], U8, name="xscale", tag="xscale", bufs=3, align_bytes=64)
+            nc.vector.quantize_mx(out=codes[g][:].bitcast(FP8X4), scales=xscale[g][:], in_=grouped[g][:])
+
+        def mx_pass(out, g, b, lo, hi):
+            nc.tensor.matmul_mx(
+                out=out,
+                lhsT=codes[g][:, b * P : (b + 1) * P].bitcast(FP8X4),
+                lhsT_scale=xscale[g][:, b * P : (b + 1) * P],
+                rhs=wcodes[:, lo:hi].bitcast(FP8X4),
+                rhs_scale=wscale[:, lo:hi],
+                start=True,
+                stop=True,
+            )
+
+        def mm_qk(s):
+            g, q = divmod(s, NBANK)
+            acc[s] = psum.tile([P, 2, NQK], F32, name="acc", tag="acc", bufs=3)
+            for tt in range(2):
+                mx_pass(acc[s][:, tt, :], g, q * 2 + tt, 0, NQK)
+
+        def mm_v(h):
+            g, hb = divmod(h, 2)
+            vacc[h] = psum.tile([P, 4, NV], F32, name="vacc", tag="vacc", bufs=1)
+            for bb in range(4):
+                mx_pass(vacc[h][:, bb, :], g, hb * 4 + bb, NQK, NQK + NV)
+
+        def exit_v(h):
+            g, hb = divmod(h, 2)
+            if hb == 0:
+                vsb[g] = work.tile([P, B, NV], F32, name="vsb", tag="vsb", bufs=2)
+            nc.scalar.copy(out=vsb[g][:, hb * 4 : (hb + 1) * 4, :], in_=vacc[h][:])
+            if hb == 1:
+                nc.sync.dma_start(out=outs_view[2][g], in_=vsb[g][:])
+
+        def sin_product(s):
+            g = s // NBANK
+            h = s // 2
+            rot_b = rot[:, g * HALF : (g + 1) * HALF, :].unsqueeze(1).to_broadcast([P, 2 * GG, HALF, 2])
+            if s % 2 == 0:
+                t1[h] = work.tile([P, 2, 2 * GG, HALF, 2], F32, name="t1", tag="t1", bufs=3)
+                t2[h] = work.tile([P, 2, 2 * GG, HALF, 2], F32, name="t2", tag="t2", bufs=3)
+            acc4 = acc[s][:].rearrange("p t (gg j two) -> p (t gg) j two", gg=GG, two=2)
+            nc.vector.tensor_tensor(out=t2[h][:, s % 2], in0=acc4[:, :, :, ::-1], in1=rot_b, op=MULT)
+
+        def cos_product(s):
+            g, q = divmod(s, NBANK)
+            h = s // 2
+            cos_b = cos2[:, g * HALF : (g + 1) * HALF, :].unsqueeze(1).to_broadcast([P, 2 * GG, HALF, 2])
+            acc4 = acc[s][:].rearrange("p t (gg j two) -> p (t gg) j two", gg=GG, two=2)
+            t1s = t1[h][:, s % 2]
+            if COS_ENGINE[q] == "gpsimd" and s < TAIL:
+                qsb = work.tile([P, 2 * GG, HALF, 2], F32, name="qsb", tag="qsb", bufs=3)
+                nc.scalar.copy(out=qsb[:], in_=acc4)
+                nc.gpsimd.tensor_tensor(out=t1s, in0=qsb[:], in1=cos_b, op=MULT)
+            elif COS_ENGINE[q] == "scalar" and s < TAIL + 2:
+                for j in range(HALF):
+                    nc.scalar.activation(
+                        out=t1s[:, :, j, :],
+                        in_=acc4[:, :, j, :],
+                        func=COPY,
+                        scale=cos2[:, g * HALF + j, 0:1],
+                    )
+            else:
+                nc.vector.tensor_tensor(out=t1s, in0=acc4, in1=cos_b, op=MULT)
+
+        def add_and_store(s):
+            g, q = divmod(s, NBANK)
+            h = s // 2
+            if q == 0:
+                y[g] = work.tile([P, B, NQK], F32, name="y", tag="y", bufs=3)
+            if h == NSTEP // 2 - 1:
+                nc.vector.tensor_tensor(
+                    out=y[g][:, q * 2 : (q + 1) * 2, :].rearrange("p t (gg j two) -> p (t gg) j two", gg=GG, two=2),
+                    in0=t1[h][:, s % 2],
+                    in1=t2[h][:, s % 2],
+                    op=ADD,
+                )
+                lo, hi = q * 2, q * 2 + 2
+            elif s % 2 == 1:
+                add_engine = nc.vector if h == NSTEP // 2 - 2 else nc.gpsimd
+                add_engine.tensor_tensor(
+                    out=y[g][:, (q - 1) * 2 : (q + 1) * 2, :].rearrange(
+                        "p t (gg j two) -> p (t gg) j two", gg=GG, two=2
+                    ),
+                    in0=t1[h][:].rearrange("p a c j two -> p (a c) j two"),
+                    in1=t2[h][:].rearrange("p a c j two -> p (a c) j two"),
+                    op=ADD,
+                )
+                lo, hi = (q - 1) * 2, q * 2 + 2
+            else:
+                return
+            if g == NG - 1:
+                for qk in range(2):
+                    nc.sync.dma_start(
+                        out=outs_view[qk][g][:, lo:hi, :], in_=y[g][:, lo:hi, qk * 128 : (qk + 1) * 128]
+                    )
+            elif q == NBANK - 1:
+                for qk in range(2):
+                    nc.sync.dma_start(out=outs_view[qk][g], in_=y[g][:, :, qk * 128 : (qk + 1) * 128])
+
+        with tc.manual_schedule():
+            nc.vector.quantize_mx(
+                out=wcodes[:, 0:NQK].bitcast(FP8X4), scales=wscale[:, 0:NQK], in_=w_flat[:, 0 : 4 * NQK]
+            )
+            nc.vector.quantize_mx(
+                out=wcodes[:, NQK : NQK + NV].bitcast(FP8X4),
+                scales=wscale[:, NQK : NQK + NV],
+                in_=w_flat[:, 4 * NQK : 4 * (NQK + NV)],
+            )
+            for i in range(-9, NSTEP):
+                if i + 9 < NSTEP:
+                    cast(i + 9)
+                if i % 2 == 1:
+                    for s in (i + 7, i + 8):
+                        if 0 <= s < NSTEP:
+                            transposes(s)
+                if 0 <= i + 6 < NSTEP:
+                    exit_scale(i + 6)
+                if i >= 0:
+                    sin_product(i)
+                if (i + 1) % 4 == 0 and 0 <= (i + 1) // 4 < NG:
+                    quantize((i + 1) // 4)
+                if i % 2 == 1:
+                    for s in (i + 1, i + 2):
+                        if 0 <= s < NSTEP:
+                            mm_qk(s)
+                    if 0 <= i + 1 < NSTEP:
+                        mm_v((i + 1) // 2)
+                if i >= 0:
+                    cos_product(i)
+                    add_and_store(i)
+                    if i % 2 == 0:
+                        exit_v(i // 2)

@@ -11,6 +11,7 @@ FP8 = mybir.dt.float8_e4m3fn
 FP8X4 = mybir.dt.float8_e4m3fn_x4
 MULT = mybir.AluOpType.mult
 ADD = mybir.AluOpType.add
+SUB = mybir.AluOpType.subtract
 COPY = mybir.ActivationFunctionType.Copy
 
 B, S, D = 8, 1024, 512
@@ -23,8 +24,10 @@ NV = 128
 GG = 4
 NBANK = B // 2
 NSTEP = NG * NBANK
-COS_ENGINE = ("gpsimd", "vector", "scalar", "vector")
-TAIL = NSTEP - 6
+NHALF = NSTEP // 2
+EV = NQK + NV
+OD = EV + 128
+NW = OD + 128
 
 FLOPS = 2 * B * S * D * (NQK + NV)
 
@@ -69,26 +72,34 @@ def tile_attention_pa_t_kernel(
         ident = const.tile([P, P], F32, name="ident")
         make_identity(nc, ident[:])
 
-        w_grouped = const.tile([P, 3, 128, 4], BF16, name="w_grouped", align_bytes=64)
-        nc.vector.tensor_copy(out=w_grouped[:], in_=w_raw[:].rearrange("p m t n -> p m n t"))
+        w_grouped = const.tile([P, 5, 128, 4], BF16, name="w_grouped", align_bytes=64)
+        nc.vector.tensor_copy(out=w_grouped[:, 0:3], in_=w_raw[:].rearrange("p m t n -> p m n t"))
+        for two in range(2):
+            for m in range(2):
+                nc.vector.tensor_copy(
+                    out=w_grouped[:, 3 + two, m * 64 : (m + 1) * 64, :],
+                    in_=w_raw[:, m, :, two::2].rearrange("p t c -> p c t"),
+                )
         w_flat = w_grouped[:].rearrange("p m n t -> p (m n t)")
-        wcodes = const.tile([P, NQK + NV], U32, name="wcodes", align_bytes=64)
-        wscale = const.tile([P, NQK + NV], U8, name="wscale", align_bytes=64)
+        wcodes = const.tile([P, NW], U32, name="wcodes", align_bytes=64)
+        wscale = const.tile([P, NW], U8, name="wscale", align_bytes=64)
 
-        cos2 = const.tile([P, NG * HALF, 2], F32, name="cos2")
+        cosf = const.tile([P, NG * HALF], F32, name="cosf")
+        csum = const.tile([P, NG * HALF], F32, name="csum")
         rot = const.tile([P, NG * HALF, 2], F32, name="rot")
         cos_flat = cos_raw[:].rearrange("p g j -> p (g j)")
         sin_flat = sin_raw[:].rearrange("p g j -> p (g j)")
-        nc.gpsimd.tensor_copy(out=cos2[:], in_=cos_flat.unsqueeze(2).to_broadcast([P, NG * HALF, 2]))
-        nc.gpsimd.tensor_scalar(out=rot[:, :, 0], in0=sin_flat, scalar1=-1.0, scalar2=0.0, op0=MULT, op1=ADD)
-        nc.gpsimd.tensor_copy(out=rot[:, :, 1], in_=sin_flat)
+        nc.gpsimd.tensor_copy(out=cosf[:], in_=cos_flat)
+        nc.gpsimd.tensor_tensor(out=csum[:], in0=cos_flat, in1=sin_flat, op=ADD)
+        nc.gpsimd.tensor_scalar(out=rot[:, :, 0], in0=csum[:], scalar1=-1.0, scalar2=0.0, op0=MULT, op1=ADD)
+        nc.gpsimd.tensor_tensor(out=rot[:, :, 1], in0=sin_flat, in1=cos_flat, op=SUB)
 
         outs_view = []
         for o in (out_0, out_1, out_2):
             outs_view.append(o.rearrange("b (g p) h d -> g p b (h d)", p=P))
         sck_b = sck[:].rearrange("p (u e) -> p u e", u=2).unsqueeze(1).to_broadcast([P, 2 * P, 2, 2])
 
-        xs, xt, grouped, codes, xscale, acc, vacc, t1, t2, y, vsb = {}, {}, {}, {}, {}, {}, {}, {}, {}, {}, {}
+        xs, xt, grouped, codes, xscale, acc, vacc, pacc, k1, t2, y, vsb = {}, {}, {}, {}, {}, {}, {}, {}, {}, {}, {}, {}
 
         def cast(s):
             g, q = divmod(s, NBANK)
@@ -97,7 +108,7 @@ def tile_attention_pa_t_kernel(
             nc.scalar.copy(out=xs[s][:], in_=xb_flat[:, q * 2 * D : (q + 1) * 2 * D].bitcast(FP8))
 
         def transposes(s):
-            xt[s] = psum.tile([P, 2, 2, P], F32, name="xt", tag="xt", bufs=4)
+            xt[s] = psum.tile([P, 2, 2, P], F32, name="xt", tag="xt", bufs=3)
             words = xs[s][:].bitcast(F32)
             for tt in range(2):
                 for u in range(2):
@@ -119,15 +130,15 @@ def tile_attention_pa_t_kernel(
             xscale[g] = work.tile([P, B * P], U8, name="xscale", tag="xscale", bufs=3, align_bytes=64)
             nc.vector.quantize_mx(out=codes[g][:].bitcast(FP8X4), scales=xscale[g][:], in_=grouped[g][:])
 
-        def mx_pass(out, g, b, lo, hi):
+        def mx_pass(out, g, b, lo, hi, start=True, stop=True):
             nc.tensor.matmul_mx(
                 out=out,
                 lhsT=codes[g][:, b * P : (b + 1) * P].bitcast(FP8X4),
                 lhsT_scale=xscale[g][:, b * P : (b + 1) * P],
                 rhs=wcodes[:, lo:hi].bitcast(FP8X4),
                 rhs_scale=wscale[:, lo:hi],
-                start=True,
-                stop=True,
+                start=start,
+                stop=stop,
             )
 
         def mm_qk(s):
@@ -150,58 +161,67 @@ def tile_attention_pa_t_kernel(
             if hb == 1:
                 nc.sync.dma_start(out=outs_view[2][g], in_=vsb[g][:])
 
-        def sin_product(s):
+        def mm_p(h):
+            g, hb = divmod(h, 2)
+            pacc[h] = psum.tile([P, 4, 128], F32, name="pacc", tag="pacc", bufs=1)
+            for bb in range(4):
+                mx_pass(pacc[h][:, bb, :], g, hb * 4 + bb, EV, EV + 128, start=True, stop=False)
+                mx_pass(pacc[h][:, bb, :], g, hb * 4 + bb, OD, OD + 128, start=False, stop=True)
+
+        def cross_product(s):
             g = s // NBANK
             h = s // 2
             rot_b = rot[:, g * HALF : (g + 1) * HALF, :].unsqueeze(1).to_broadcast([P, 2 * GG, HALF, 2])
             if s % 2 == 0:
-                t1[h] = work.tile([P, 2, 2 * GG, HALF, 2], F32, name="t1", tag="t1", bufs=3)
                 t2[h] = work.tile([P, 2, 2 * GG, HALF, 2], F32, name="t2", tag="t2", bufs=3)
             acc4 = acc[s][:].rearrange("p t (gg j two) -> p (t gg) j two", gg=GG, two=2)
             nc.vector.tensor_tensor(out=t2[h][:, s % 2], in0=acc4[:, :, :, ::-1], in1=rot_b, op=MULT)
 
-        def cos_product(s):
-            g, q = divmod(s, NBANK)
-            h = s // 2
-            cos_b = cos2[:, g * HALF : (g + 1) * HALF, :].unsqueeze(1).to_broadcast([P, 2 * GG, HALF, 2])
-            acc4 = acc[s][:].rearrange("p t (gg j two) -> p (t gg) j two", gg=GG, two=2)
-            t1s = t1[h][:, s % 2]
-            if COS_ENGINE[q] == "gpsimd" and s < TAIL:
-                qsb = work.tile([P, 2 * GG, HALF, 2], F32, name="qsb", tag="qsb", bufs=3)
-                nc.scalar.copy(out=qsb[:], in_=acc4)
-                nc.gpsimd.tensor_tensor(out=t1s, in0=qsb[:], in1=cos_b, op=MULT)
-            elif COS_ENGINE[q] == "scalar" and s < TAIL + 2:
+        def on_scalar(h):
+            return h % 2 == 0
+
+        def cos_product(h):
+            g = h // 2
+            pv = pacc[h][:].rearrange("p t (gg j) -> p (t gg) j", gg=GG)
+            if on_scalar(h):
+                k1[h] = work.tile([P, HALF, 4 * GG], F32, name="k1s", tag="k1s", bufs=2)
                 for j in range(HALF):
                     nc.scalar.activation(
-                        out=t1s[:, :, j, :],
-                        in_=acc4[:, :, j, :],
+                        out=k1[h][:, j, :],
+                        in_=pv[:, :, j],
                         func=COPY,
-                        scale=cos2[:, g * HALF + j, 0:1],
+                        scale=cosf[:, g * HALF + j : g * HALF + j + 1],
                     )
             else:
-                nc.vector.tensor_tensor(out=t1s, in0=acc4, in1=cos_b, op=MULT)
+                k1[h] = work.tile([P, 4 * GG, HALF], F32, name="k1v", tag="k1v", bufs=2)
+                cos_b = cosf[:, g * HALF : (g + 1) * HALF].unsqueeze(1).to_broadcast([P, 4 * GG, HALF])
+                nc.vector.tensor_tensor(out=k1[h][:], in0=pv, in1=cos_b, op=MULT)
+
+        def k1_view(h, lo, hi):
+            v = k1[h][:].rearrange("p j c -> p c j") if on_scalar(h) else k1[h][:]
+            return v[:, lo:hi, :].unsqueeze(3).to_broadcast([P, hi - lo, HALF, 2])
 
         def add_and_store(s):
             g, q = divmod(s, NBANK)
             h = s // 2
             if q == 0:
                 y[g] = work.tile([P, B, NQK], F32, name="y", tag="y", bufs=3)
-            if h == NSTEP // 2 - 1:
+            if h == NHALF - 1:
                 nc.vector.tensor_tensor(
                     out=y[g][:, q * 2 : (q + 1) * 2, :].rearrange("p t (gg j two) -> p (t gg) j two", gg=GG, two=2),
-                    in0=t1[h][:, s % 2],
-                    in1=t2[h][:, s % 2],
+                    in0=t2[h][:, s % 2],
+                    in1=k1_view(h, (s % 2) * 2 * GG, (s % 2 + 1) * 2 * GG),
                     op=ADD,
                 )
                 lo, hi = q * 2, q * 2 + 2
             elif s % 2 == 1:
-                add_engine = nc.vector if h == NSTEP // 2 - 2 else nc.gpsimd
+                add_engine = nc.vector if h == NHALF - 2 else nc.gpsimd
                 add_engine.tensor_tensor(
                     out=y[g][:, (q - 1) * 2 : (q + 1) * 2, :].rearrange(
                         "p t (gg j two) -> p (t gg) j two", gg=GG, two=2
                     ),
-                    in0=t1[h][:].rearrange("p a c j two -> p (a c) j two"),
-                    in1=t2[h][:].rearrange("p a c j two -> p (a c) j two"),
+                    in0=t2[h][:].rearrange("p a c j two -> p (a c) j two"),
+                    in1=k1_view(h, 0, 4 * GG),
                     op=ADD,
                 )
                 lo, hi = (q - 1) * 2, q * 2 + 2
@@ -217,14 +237,10 @@ def tile_attention_pa_t_kernel(
                     nc.sync.dma_start(out=outs_view[qk][g], in_=y[g][:, :, qk * 128 : (qk + 1) * 128])
 
         with tc.manual_schedule():
-            nc.vector.quantize_mx(
-                out=wcodes[:, 0:NQK].bitcast(FP8X4), scales=wscale[:, 0:NQK], in_=w_flat[:, 0 : 4 * NQK]
-            )
-            nc.vector.quantize_mx(
-                out=wcodes[:, NQK : NQK + NV].bitcast(FP8X4),
-                scales=wscale[:, NQK : NQK + NV],
-                in_=w_flat[:, 4 * NQK : 4 * (NQK + NV)],
-            )
+            for lo, hi in ((0, NQK), (NQK, EV), (EV, NW)):
+                nc.vector.quantize_mx(
+                    out=wcodes[:, lo:hi].bitcast(FP8X4), scales=wscale[:, lo:hi], in_=w_flat[:, 4 * lo : 4 * hi]
+                )
             for i in range(-9, NSTEP):
                 if i + 9 < NSTEP:
                     cast(i + 9)
@@ -234,18 +250,19 @@ def tile_attention_pa_t_kernel(
                             transposes(s)
                 if 0 <= i + 6 < NSTEP:
                     exit_scale(i + 6)
-                if i >= 0:
-                    sin_product(i)
                 if (i + 1) % 4 == 0 and 0 <= (i + 1) // 4 < NG:
                     quantize((i + 1) // 4)
+                if i >= 0:
+                    cross_product(i)
+                    if i % 2 == 0:
+                        exit_v(i // 2)
+                        cos_product(i // 2)
                 if i % 2 == 1:
                     for s in (i + 1, i + 2):
                         if 0 <= s < NSTEP:
                             mm_qk(s)
                     if 0 <= i + 1 < NSTEP:
                         mm_v((i + 1) // 2)
+                        mm_p((i + 1) // 2)
                 if i >= 0:
-                    cos_product(i)
                     add_and_store(i)
-                    if i % 2 == 0:
-                        exit_v(i // 2)

@@ -103,7 +103,7 @@ def tile_attention_pa_t_kernel(
 
         def cast(s):
             g, q = divmod(s, NBANK)
-            xs[s] = work.tile([P, 2 * D], BF16, name="xs", tag="xs", bufs=4)
+            xs[s] = work.tile([P, 2 * D], BF16, name="xs", tag="xs", bufs=6)
             xb_flat = xbytes[g][:].rearrange("p b k -> p (b k)")
             nc.scalar.copy(out=xs[s][:], in_=xb_flat[:, q * 2 * D : (q + 1) * 2 * D].bitcast(FP8))
 
@@ -178,7 +178,7 @@ def tile_attention_pa_t_kernel(
             nc.vector.tensor_tensor(out=t2[h][:, s % 2], in0=acc4[:, :, :, ::-1], in1=rot_b, op=MULT)
 
         def on_scalar(h):
-            return h % 2 == 0
+            return h % 2 == 0 and h < NHALF - 2
 
         def cos_product(h):
             g = h // 2
@@ -250,19 +250,24 @@ def tile_attention_pa_t_kernel(
                             transposes(s)
                 if 0 <= i + 6 < NSTEP:
                     exit_scale(i + 6)
-                if (i + 1) % 4 == 0 and 0 <= (i + 1) // 4 < NG:
-                    quantize((i + 1) // 4)
+                h = i // 2
                 if i >= 0:
                     cross_product(i)
-                    if i % 2 == 0:
-                        exit_v(i // 2)
-                        cos_product(i // 2)
+                if (i + 1) % 4 == 0 and 0 <= (i + 1) // 4 < NG:
+                    quantize((i + 1) // 4)
+                if i >= 0 and i % 2 == 0:
+                    exit_v(h)
+                    if on_scalar(h) or h == NHALF - 1:
+                        cos_product(h)
                 if i % 2 == 1:
                     for s in (i + 1, i + 2):
                         if 0 <= s < NSTEP:
                             mm_qk(s)
                     if 0 <= i + 1 < NSTEP:
-                        mm_v((i + 1) // 2)
-                        mm_p((i + 1) // 2)
+                        mm_v(h + 1)
+                    if i >= 0 and not on_scalar(h) and h < NHALF - 1:
+                        cos_product(h)
+                    if 0 <= i + 1 < NSTEP:
+                        mm_p(h + 1)
                 if i >= 0:
                     add_and_store(i)

@@ -73,7 +73,11 @@ def tile_attention_pa_t_kernel(
         make_identity(nc, ident[:])
 
         w_grouped = const.tile([P, 5, 128, 4], BF16, name="w_grouped", align_bytes=64)
-        nc.vector.tensor_copy(out=w_grouped[:, 0:3], in_=w_raw[:].rearrange("p m t n -> p m n t"))
+        for two in range(2):
+            nc.vector.tensor_copy(
+                out=w_grouped[:, 0:2, two::2, :], in_=w_raw[:, 0:2, :, 1 - two :: 2].rearrange("p m t c -> p m c t")
+            )
+        nc.vector.tensor_copy(out=w_grouped[:, 2], in_=w_raw[:, 2].rearrange("p t n -> p n t"))
         for two in range(2):
             for m in range(2):
                 nc.vector.tensor_copy(
@@ -175,7 +179,7 @@ def tile_attention_pa_t_kernel(
             if s % 2 == 0:
                 t2[h] = work.tile([P, 2, 2 * GG, HALF, 2], F32, name="t2", tag="t2", bufs=3)
             acc4 = acc[s][:].rearrange("p t (gg j two) -> p (t gg) j two", gg=GG, two=2)
-            nc.vector.tensor_tensor(out=t2[h][:, s % 2], in0=acc4[:, :, :, ::-1], in1=rot_b, op=MULT)
+            nc.vector.tensor_tensor(out=t2[h][:, s % 2], in0=acc4, in1=rot_b, op=MULT)
 
         def on_scalar(h):
             return h % 2 == 0 and h < NHALF - 2

@@ -182,7 +182,7 @@ def tile_attention_pa_t_kernel(
             nc.vector.tensor_tensor(out=t2[h][:, s % 2], in0=acc4, in1=rot_b, op=MULT)
 
         def on_scalar(h):
-            return h % 2 == 0 and h < NHALF - 2
+            return h % 2 == 1 and h < NHALF - 1
 
         def cos_product(h):
             g = h // 2
@@ -245,33 +245,51 @@ def tile_attention_pa_t_kernel(
                 nc.vector.quantize_mx(
                     out=wcodes[:, lo:hi].bitcast(FP8X4), scales=wscale[:, lo:hi], in_=w_flat[:, 4 * lo : 4 * hi]
                 )
-            for i in range(-9, NSTEP):
-                if i + 9 < NSTEP:
-                    cast(i + 9)
-                if i % 2 == 1:
-                    for s in (i + 7, i + 8):
-                        if 0 <= s < NSTEP:
-                            transposes(s)
-                if 0 <= i + 6 < NSTEP:
-                    exit_scale(i + 6)
-                h = i // 2
-                if i >= 0:
-                    cross_product(i)
-                if (i + 1) % 4 == 0 and 0 <= (i + 1) // 4 < NG:
-                    quantize((i + 1) // 4)
-                if i >= 0 and i % 2 == 0:
-                    exit_v(h)
-                    if on_scalar(h) or h == NHALF - 1:
-                        cos_product(h)
-                if i % 2 == 1:
-                    for s in (i + 1, i + 2):
-                        if 0 <= s < NSTEP:
-                            mm_qk(s)
-                    if 0 <= i + 1 < NSTEP:
-                        mm_v(h + 1)
-                    if i >= 0 and not on_scalar(h) and h < NHALF - 1:
-                        cos_product(h)
-                    if 0 <= i + 1 < NSTEP:
-                        mm_p(h + 1)
-                if i >= 0:
-                    add_and_store(i)
+            def guarded(fn, n, x):
+                if 0 <= x < n:
+                    fn(x)
+
+            for g in range(-3, NG):
+                s0 = NBANK * g
+                ha, hb = 2 * g, 2 * g + 1
+                last = g == NG - 1
+                guarded(cast, NSTEP, s0 + 10)
+                guarded(exit_scale, NSTEP, s0 + 6)
+                guarded(cross_product, NSTEP, s0)
+                guarded(cross_product, NSTEP, s0 + 1)
+                guarded(exit_v, NHALF, ha)
+                guarded(cos_product, NHALF, ha)
+                if not last:
+                    guarded(add_and_store, NSTEP, s0)
+                    guarded(add_and_store, NSTEP, s0 + 1)
+                guarded(cast, NSTEP, s0 + 11)
+                guarded(transposes, NSTEP, s0 + 8)
+                guarded(transposes, NSTEP, s0 + 9)
+                guarded(mm_qk, NSTEP, s0 + 2)
+                guarded(mm_qk, NSTEP, s0 + 3)
+                guarded(mm_v, NHALF, hb)
+                guarded(mm_p, NHALF, hb)
+                guarded(exit_scale, NSTEP, s0 + 7)
+                guarded(exit_scale, NSTEP, s0 + 8)
+                guarded(cast, NSTEP, s0 + 12)
+                guarded(cross_product, NSTEP, s0 + 2)
+                guarded(exit_v, NHALF, hb)
+                if not last:
+                    guarded(cos_product, NHALF, hb)
+                guarded(exit_scale, NSTEP, s0 + 9)
+                guarded(cast, NSTEP, s0 + 13)
+                guarded(quantize, NG, g + 1)
+                guarded(transposes, NSTEP, s0 + 10)
+                guarded(transposes, NSTEP, s0 + 11)
+                guarded(mm_qk, NSTEP, s0 + 4)
+                guarded(mm_qk, NSTEP, s0 + 5)
+                guarded(mm_p, NHALF, ha + 2)
+                guarded(mm_v, NHALF, ha + 2)
+                guarded(cross_product, NSTEP, s0 + 3)
+                if last:
+                    cos_product(hb)
+                    for s in range(s0, s0 + 4):
+                        add_and_store(s)
+                else:
+                    guarded(add_and_store, NSTEP, s0 + 2)
+                    guarded(add_and_store, NSTEP, s0 + 3)

@@ -162,7 +162,11 @@ def tile_attention_pa_t_kernel(
             if hb == 0:
                 vsb[g] = work.tile([P, B, NV], F32, name="vsb", tag="vsb", bufs=2)
             nc.scalar.copy(out=vsb[g][:, hb * 4 : (hb + 1) * 4, :], in_=vacc[h][:])
-            if hb == 1:
+            if g >= NG - 2:
+                nc.sync.dma_start(
+                    out=outs_view[2][g][:, hb * 4 : (hb + 1) * 4, :], in_=vsb[g][:, hb * 4 : (hb + 1) * 4, :]
+                )
+            elif hb == 1:
                 nc.sync.dma_start(out=outs_view[2][g], in_=vsb[g][:])
 
         def mm_p(h):
@@ -182,13 +186,13 @@ def tile_attention_pa_t_kernel(
             nc.vector.tensor_tensor(out=t2[h][:, s % 2], in0=acc4, in1=rot_b, op=MULT)
 
         def on_scalar(h):
-            return h % 2 == 1 and h < NHALF - 1
+            return (h % 2 == 1 and h < NHALF - 1) or (h % 4 == 2 and h < NHALF - 2)
 
         def cos_product(h):
             g = h // 2
             pv = pacc[h][:].rearrange("p t (gg j) -> p (t gg) j", gg=GG)
             if on_scalar(h):
-                k1[h] = work.tile([P, HALF, 4 * GG], F32, name="k1s", tag="k1s", bufs=2)
+                k1[h] = work.tile([P, HALF, 4 * GG], F32, name="k1s", tag="k1s", bufs=3)
                 for j in range(HALF):
                     nc.scalar.activation(
                         out=k1[h][:, j, :],
@@ -231,7 +235,7 @@ def tile_attention_pa_t_kernel(
                 lo, hi = (q - 1) * 2, q * 2 + 2
             else:
                 return
-            if g == NG - 1:
+            if g >= NG - 2:
                 for qk in range(2):
                     nc.sync.dma_start(
                         out=outs_view[qk][g][:, lo:hi, :], in_=y[g][:, lo:hi, qk * 128 : (qk + 1) * 128]
@@ -253,12 +257,15 @@ def tile_attention_pa_t_kernel(
                 s0 = NBANK * g
                 ha, hb = 2 * g, 2 * g + 1
                 last = g == NG - 1
+                if 0 <= ha < NHALF and on_scalar(ha):
+                    cos_product(ha)
                 guarded(cast, NSTEP, s0 + 10)
                 guarded(exit_scale, NSTEP, s0 + 6)
                 guarded(cross_product, NSTEP, s0)
                 guarded(cross_product, NSTEP, s0 + 1)
                 guarded(exit_v, NHALF, ha)
-                guarded(cos_product, NHALF, ha)
+                if 0 <= ha < NHALF and not on_scalar(ha):
+                    cos_product(ha)
                 if not last:
                     guarded(add_and_store, NSTEP, s0)
                     guarded(add_and_store, NSTEP, s0 + 1)

@@ -101,7 +101,7 @@ def tile_attention_pa_t_kernel(
         outs_view = []
         for o in (out_0, out_1, out_2):
             outs_view.append(o.rearrange("b (g p) h d -> g p b (h d)", p=P))
-        sck_b = sck[:].rearrange("p (u e) -> p u e", u=2).unsqueeze(1).to_broadcast([P, 2 * P, 2, 2])
+        sck_b = sck[:].unsqueeze(1).to_broadcast([P, 2 * P, 4])
 
         xs, xt, grouped, codes, xscale, acc, vacc, pacc, k1, t2, y, vsb = {}, {}, {}, {}, {}, {}, {}, {}, {}, {}, {}, {}
 
@@ -112,19 +112,19 @@ def tile_attention_pa_t_kernel(
             nc.scalar.copy(out=xs[s][:], in_=xb_flat[:, q * 2 * D : (q + 1) * 2 * D].bitcast(FP8))
 
         def transposes(s):
-            xt[s] = psum.tile([P, 2, 2, P], F32, name="xt", tag="xt", bufs=3)
+            xt[s] = psum.tile([P, 2, P, 2], F32, name="xt", tag="xt", bufs=3)
             words = xs[s][:].bitcast(F32)
             for tt in range(2):
                 for u in range(2):
-                    nc.tensor.transpose(xt[s][:, u, tt, :], words[:, tt * 256 + u : (tt + 1) * 256 : 2], ident[:])
+                    nc.tensor.transpose(xt[s][:, tt, :, u], words[:, tt * 256 + u : (tt + 1) * 256 : 2], ident[:])
 
         def exit_scale(s):
             g, q = divmod(s, NBANK)
             if q == 0:
                 grouped[g] = work.tile([P, B * P * 4], BF16, name="grouped", tag="grouped", bufs=3, align_bytes=64)
             nc.vector.tensor_tensor(
-                out=grouped[g][:, q * 8 * P : (q + 1) * 8 * P].rearrange("p (r u e) -> p r u e", u=2, e=2),
-                in0=xt[s][:].bitcast(BF16).rearrange("p u t (r e) -> p (t r) u e", e=2),
+                out=grouped[g][:, q * 8 * P : (q + 1) * 8 * P].rearrange("p (r k) -> p r k", k=4),
+                in0=xt[s][:].rearrange("p t r u -> p (t r u)").bitcast(BF16).rearrange("p (r k) -> p r k", k=4),
                 in1=sck_b,
                 op=MULT,
             )

@@ -60,14 +60,15 @@ def tile_attention_pa_t_kernel(
         for m, w in enumerate((wq, wk, wv)):
             nc.sync.dma_start(out=w_raw[:, m], in_=w.rearrange("(p t) n -> p t n", t=4))
         nc.sync.dma_start(out=xbytes[0][:, 4:8, :], in_=x_view[0][:, 4:8, :])
-        nc.sync.dma_start(
-            out=cos_raw[:], in_=freq_cos.rearrange("a s c j -> (a s) (c j)").rearrange("(g p) j -> p g j", p=P)
-        )
-        nc.sync.dma_start(
-            out=sin_raw[:], in_=freq_sin.rearrange("a s c j -> (a s) (c j)").rearrange("(g p) j -> p g j", p=P)
-        )
         for g in range(1, NG):
             nc.sync.dma_start(out=xbytes[g][:], in_=x_view[g])
+            if g == 2:
+                nc.sync.dma_start(
+                    out=cos_raw[:], in_=freq_cos.rearrange("a s c j -> (a s) (c j)").rearrange("(g p) j -> p g j", p=P)
+                )
+                nc.sync.dma_start(
+                    out=sin_raw[:], in_=freq_sin.rearrange("a s c j -> (a s) (c j)").rearrange("(g p) j -> p g j", p=P)
+                )
 
         ident = const.tile([P, P], F32, name="ident")
         make_identity(nc, ident[:])

from contextlib import ExitStack

import concourse.mybir as mybir
from concourse.masks import make_identity

F32 = mybir.dt.float32
BF16 = mybir.dt.bfloat16
U32 = mybir.dt.uint32
U8 = mybir.dt.uint8
FP8 = mybir.dt.float8_e4m3fn
FP8X4 = mybir.dt.float8_e4m3fn_x4
MULT = mybir.AluOpType.mult
ADD = mybir.AluOpType.add
SUB = mybir.AluOpType.subtract
COPY = mybir.ActivationFunctionType.Copy

B, S, D = 8, 1024, 512
HEADS, HD = 2, 64
HALF = HD // 2
P = 128
NG = S // P
NQK = 256
NV = 128
GG = 4
NBANK = B // 2
NSTEP = NG * NBANK
NHALF = NSTEP // 2
EV = NQK + NV
OD = EV + 128
NW = OD + 128

FLOPS = 2 * B * S * D * (NQK + NV)


def tile_attention_pa_t_kernel(
    tc, hidden_state_bytes, hidden_state_scale, freq_cos, freq_sin, wq, wk, wv, out_0, out_1, out_2
):
    nc = tc.nc
    with ExitStack() as ctx:
        const = ctx.enter_context(tc.tile_pool(name="const", bufs=1))
        work = ctx.enter_context(tc.tile_pool(name="work", bufs=2))
        psum = ctx.enter_context(tc.psum_pool(name="psum", bufs=2))

        warm = const.tile([P, 2], F32, name="warm")
        nc.vector.memset(warm[:, 0:1], 0.0)
        nc.scalar.copy(out=warm[:, 1:2], in_=warm[:, 0:1])

        x_view = hidden_state_bytes.rearrange("b (g p) k -> g p b k", p=P)
        xbytes = []
        for g in range(NG):
            xb = const.tile([P, B, D], U8, name="xbytes%d" % g)
            xbytes.append(xb)
        sck = const.tile([P, 4], F32, name="sck")
        w_raw = const.tile([P, 3, 4, 128], BF16, name="w_raw")
        cos_raw = const.tile([P, NG, HALF], BF16, name="cos_raw")
        sin_raw = const.tile([P, NG, HALF], BF16, name="sin_raw")
        nc.sync.dma_start(out=xbytes[0][:, 0:2, :], in_=x_view[0][:, 0:2, :])
        nc.sync.dma_start(out=sck[:], in_=hidden_state_scale.rearrange("a b (p t) -> (a b p) t", t=4))
        nc.sync.dma_start(out=xbytes[0][:, 2:4, :], in_=x_view[0][:, 2:4, :])
        for m, w in enumerate((wq, wk, wv)):
            nc.sync.dma_start(out=w_raw[:, m], in_=w.rearrange("(p t) n -> p t n", t=4))
        nc.sync.dma_start(out=xbytes[0][:, 4:8, :], in_=x_view[0][:, 4:8, :])
        for g in range(1, NG):
            nc.sync.dma_start(out=xbytes[g][:], in_=x_view[g])
            if g == 2:
                nc.sync.dma_start(
                    out=cos_raw[:], in_=freq_cos.rearrange("a s c j -> (a s) (c j)").rearrange("(g p) j -> p g j", p=P)
                )
                nc.sync.dma_start(
                    out=sin_raw[:], in_=freq_sin.rearrange("a s c j -> (a s) (c j)").rearrange("(g p) j -> p g j", p=P)
                )

        ident = const.tile([P, P], F32, name="ident")
        make_identity(nc, ident[:])

        w_grouped = const.tile([P, 5, 128, 4], BF16, name="w_grouped", align_bytes=64)
        for two in range(2):
            nc.vector.tensor_copy(
                out=w_grouped[:, 0:2, two::2, :], in_=w_raw[:, 0:2, :, 1 - two :: 2].rearrange("p m t c -> p m c t")
            )
        nc.vector.tensor_copy(out=w_grouped[:, 2], in_=w_raw[:, 2].rearrange("p t n -> p n t"))
        for two in range(2):
            for m in range(2):
                nc.vector.tensor_copy(
                    out=w_grouped[:, 3 + two, m * 64 : (m + 1) * 64, :],
                    in_=w_raw[:, m, :, two::2].rearrange("p t c -> p c t"),
                )
        w_flat = w_grouped[:].rearrange("p m n t -> p (m n t)")
        wcodes = const.tile([P, NW], U32, name="wcodes", align_bytes=64)
        wscale = const.tile([P, NW], U8, name="wscale", align_bytes=64)

        cosf = const.tile([P, NG * HALF], F32, name="cosf")
        csum = const.tile([P, NG * HALF], F32, name="csum")
        rot = const.tile([P, NG * HALF, 2], F32, name="rot")
        cos_flat = cos_raw[:].rearrange("p g j -> p (g j)")
        sin_flat = sin_raw[:].rearrange("p g j -> p (g j)")
        nc.gpsimd.tensor_copy(out=cosf[:], in_=cos_flat)
        nc.gpsimd.tensor_tensor(out=csum[:], in0=cos_flat, in1=sin_flat, op=ADD)
        nc.gpsimd.tensor_scalar(out=rot[:, :, 0], in0=csum[:], scalar1=-1.0, scalar2=0.0, op0=MULT, op1=ADD)
        nc.gpsimd.tensor_tensor(out=rot[:, :, 1], in0=sin_flat, in1=cos_flat, op=SUB)

        outs_view = []
        for o in (out_0, out_1, out_2):
            outs_view.append(o.rearrange("b (g p) h d -> g p b (h d)", p=P))
        sck_b = sck[:].unsqueeze(1).to_broadcast([P, 2 * P, 4])

        xs, xt, grouped, codes, xscale, acc, vacc, pacc, k1, t2, y, vsb = {}, {}, {}, {}, {}, {}, {}, {}, {}, {}, {}, {}

        def cast(s):
            g, q = divmod(s, NBANK)
            xs[s] = work.tile([P, 2 * D], BF16, name="xs", tag="xs", bufs=6)
            xb_flat = xbytes[g][:].rearrange("p b k -> p (b k)")
            nc.scalar.copy(out=xs[s][:], in_=xb_flat[:, q * 2 * D : (q + 1) * 2 * D].bitcast(FP8))

        def transposes(s):
            xt[s] = psum.tile([P, 2, P, 2], F32, name="xt", tag="xt", bufs=3)
            words = xs[s][:].bitcast(F32)
            for tt in range(2):
                for u in range(2):
                    nc.tensor.transpose(xt[s][:, tt, :, u], words[:, tt * 256 + u : (tt + 1) * 256 : 2], ident[:])

        def exit_scale(s):
            g, q = divmod(s, NBANK)
            if q == 0:
                grouped[g] = work.tile([P, B * P * 4], BF16, name="grouped", tag="grouped", bufs=3, align_bytes=64)
            nc.vector.tensor_tensor(
                out=grouped[g][:, q * 8 * P : (q + 1) * 8 * P].rearrange("p (r k) -> p r k", k=4),
                in0=xt[s][:].rearrange("p t r u -> p (t r u)").bitcast(BF16).rearrange("p (r k) -> p r k", k=4),
                in1=sck_b,
                op=MULT,
            )

        def quantize(g):
            codes[g] = work.tile([P, B * P], U32, name="codes", tag="codes", bufs=3, align_bytes=64)
            xscale[g] = work.tile([P, B * P], U8, name="xscale", tag="xscale", bufs=3, align_bytes=64)
            nc.vector.quantize_mx(out=codes[g][:].bitcast(FP8X4), scales=xscale[g][:], in_=grouped[g][:])

        def mx_pass(out, g, b, lo, hi, start=True, stop=True):
            nc.tensor.matmul_mx(
                out=out,
                lhsT=codes[g][:, b * P : (b + 1) * P].bitcast(FP8X4),
                lhsT_scale=xscale[g][:, b * P : (b + 1) * P],
                rhs=wcodes[:, lo:hi].bitcast(FP8X4),
                rhs_scale=wscale[:, lo:hi],
                start=start,
                stop=stop,
            )

        def mm_qk(s):
            g, q = divmod(s, NBANK)
            acc[s] = psum.tile([P, 2, NQK], F32, name="acc", tag="acc", bufs=3)
            for tt in range(2):
                mx_pass(acc[s][:, tt, :], g, q * 2 + tt, 0, NQK)

        def mm_v(h):
            g, hb = divmod(h, 2)
            vacc[h] = psum.tile([P, 4, NV], F32, name="vacc", tag="vacc", bufs=1)
            for bb in range(4):
                mx_pass(vacc[h][:, bb, :], g, hb * 4 + bb, NQK, NQK + NV)

        def exit_v(h):
            g, hb = divmod(h, 2)
            if hb == 0:
                vsb[g] = work.tile([P, B, NV], F32, name="vsb", tag="vsb", bufs=2)
            nc.scalar.copy(out=vsb[g][:, hb * 4 : (hb + 1) * 4, :], in_=vacc[h][:])
            if g >= NG - 2:
                nc.sync.dma_start(
                    out=outs_view[2][g][:, hb * 4 : (hb + 1) * 4, :], in_=vsb[g][:, hb * 4 : (hb + 1) * 4, :]
                )
            elif hb == 1:
                nc.sync.dma_start(out=outs_view[2][g], in_=vsb[g][:])

        def mm_p(h):
            g, hb = divmod(h, 2)
            pacc[h] = psum.tile([P, 4, 128], F32, name="pacc", tag="pacc", bufs=1)
            for bb in range(4):
                mx_pass(pacc[h][:, bb, :], g, hb * 4 + bb, EV, EV + 128, start=True, stop=False)
                mx_pass(pacc[h][:, bb, :], g, hb * 4 + bb, OD, OD + 128, start=False, stop=True)

        def cross_product(s):
            g = s // NBANK
            h = s // 2
            rot_b = rot[:, g * HALF : (g + 1) * HALF, :].unsqueeze(1).to_broadcast([P, 2 * GG, HALF, 2])
            if s % 2 == 0:
                t2[h] = work.tile([P, 2, 2 * GG, HALF, 2], F32, name="t2", tag="t2", bufs=3)
            acc4 = acc[s][:].rearrange("p t (gg j two) -> p (t gg) j two", gg=GG, two=2)
            nc.vector.tensor_tensor(out=t2[h][:, s % 2], in0=acc4, in1=rot_b, op=MULT)

        def on_scalar(h):
            return (h % 2 == 1 and h < NHALF - 1) or (h % 4 == 2 and h < NHALF - 2)

        def cos_product(h):
            g = h // 2
            pv = pacc[h][:].rearrange("p t (gg j) -> p (t gg) j", gg=GG)
            if on_scalar(h):
                k1[h] = work.tile([P, HALF, 4 * GG], F32, name="k1s", tag="k1s", bufs=3)
                for j in range(HALF):
                    nc.scalar.activation(
                        out=k1[h][:, j, :],
                        in_=pv[:, :, j],
                        func=COPY,
                        scale=cosf[:, g * HALF + j : g * HALF + j + 1],
                    )
            else:
                k1[h] = work.tile([P, 4 * GG, HALF], F32, name="k1v", tag="k1v", bufs=2)
                cos_b = cosf[:, g * HALF : (g + 1) * HALF].unsqueeze(1).to_broadcast([P, 4 * GG, HALF])
                nc.vector.tensor_tensor(out=k1[h][:], in0=pv, in1=cos_b, op=MULT)

        def k1_view(h, lo, hi):
            v = k1[h][:].rearrange("p j c -> p c j") if on_scalar(h) else k1[h][:]
            return v[:, lo:hi, :].unsqueeze(3).to_broadcast([P, hi - lo, HALF, 2])

        def add_and_store(s):
            g, q = divmod(s, NBANK)
            h = s // 2
            if q == 0:
                y[g] = work.tile([P, B, NQK], F32, name="y", tag="y", bufs=3)
            if h == NHALF - 1:
                nc.vector.tensor_tensor(
                    out=y[g][:, q * 2 : (q + 1) * 2, :].rearrange("p t (gg j two) -> p (t gg) j two", gg=GG, two=2),
                    in0=t2[h][:, s % 2],
                    in1=k1_view(h, (s % 2) * 2 * GG, (s % 2 + 1) * 2 * GG),
                    op=ADD,
                )
                lo, hi = q * 2, q * 2 + 2
            elif s % 2 == 1:
                add_engine = nc.vector if h == NHALF - 2 else nc.gpsimd
                add_engine.tensor_tensor(
                    out=y[g][:, (q - 1) * 2 : (q + 1) * 2, :].rearrange(
                        "p t (gg j two) -> p (t gg) j two", gg=GG, two=2
                    ),
                    in0=t2[h][:].rearrange("p a c j two -> p (a c) j two"),
                    in1=k1_view(h, 0, 4 * GG),
                    op=ADD,
                )
                lo, hi = (q - 1) * 2, q * 2 + 2
            else:
                return
            if g >= NG - 2:
                for qk in range(2):
                    nc.sync.dma_start(
                        out=outs_view[qk][g][:, lo:hi, :], in_=y[g][:, lo:hi, qk * 128 : (qk + 1) * 128]
                    )
            elif q == NBANK - 1:
                for qk in range(2):
                    nc.sync.dma_start(out=outs_view[qk][g], in_=y[g][:, :, qk * 128 : (qk + 1) * 128])

        with tc.manual_schedule():
            for lo, hi in ((0, NQK), (NQK, EV), (EV, NW)):
                nc.vector.quantize_mx(
                    out=wcodes[:, lo:hi].bitcast(FP8X4), scales=wscale[:, lo:hi], in_=w_flat[:, 4 * lo : 4 * hi]
                )
            def guarded(fn, n, x):
                if 0 <= x < n:
                    fn(x)

            for g in range(-3, NG):
                s0 = NBANK * g
                ha, hb = 2 * g, 2 * g + 1
                last = g == NG - 1
                if 0 <= ha < NHALF and on_scalar(ha):
                    cos_product(ha)
                guarded(cast, NSTEP, s0 + 10)
                guarded(exit_scale, NSTEP, s0 + 6)
                guarded(cross_product, NSTEP, s0)
                guarded(cross_product, NSTEP, s0 + 1)
                guarded(exit_v, NHALF, ha)
                if 0 <= ha < NHALF and not on_scalar(ha):
                    cos_product(ha)
                if not last:
                    guarded(add_and_store, NSTEP, s0)
                    guarded(add_and_store, NSTEP, s0 + 1)
                guarded(cast, NSTEP, s0 + 11)
                guarded(transposes, NSTEP, s0 + 8)
                guarded(transposes, NSTEP, s0 + 9)
                guarded(mm_qk, NSTEP, s0 + 2)
                guarded(mm_qk, NSTEP, s0 + 3)
                guarded(mm_v, NHALF, hb)
                guarded(mm_p, NHALF, hb)
                guarded(exit_scale, NSTEP, s0 + 7)
                guarded(exit_scale, NSTEP, s0 + 8)
                guarded(cast, NSTEP, s0 + 12)
                guarded(cross_product, NSTEP, s0 + 2)
                guarded(exit_v, NHALF, hb)
                if not last:
                    guarded(cos_product, NHALF, hb)
                guarded(exit_scale, NSTEP, s0 + 9)
                guarded(cast, NSTEP, s0 + 13)
                guarded(quantize, NG, g + 1)
                guarded(transposes, NSTEP, s0 + 10)
                guarded(transposes, NSTEP, s0 + 11)
                guarded(mm_qk, NSTEP, s0 + 4)
                guarded(mm_qk, NSTEP, s0 + 5)
                guarded(mm_p, NHALF, ha + 2)
                guarded(mm_v, NHALF, ha + 2)
                guarded(cross_product, NSTEP, s0 + 3)
                if last:
                    cos_product(hb)
                    for s in range(s0, s0 + 4):
                        add_and_store(s)
                else:
                    guarded(add_and_store, NSTEP, s0 + 2)
                    guarded(add_and_store, NSTEP, s0 + 3)
